import numpy as np
import ml_dtypes


def mxq(x, axis, fmt="e4m3"):
    dtype, down = {"e4m3": (ml_dtypes.float8_e4m3fn, 7), "e5m2": (ml_dtypes.float8_e5m2, 14)}[fmt]
    v = np.moveaxis(np.asarray(x, np.float32).astype(ml_dtypes.bfloat16).astype(np.float64), axis, -1)
    blocks = v.reshape(v.shape[:-1] + (-1, 32))
    amax = np.abs(blocks).max(-1, keepdims=True)
    byte = np.maximum(np.where(amax > 0, np.frexp(amax)[1] - 1 + 127, 0) - down, 1)
    scale = np.exp2(byte - 127.0)
    codes = (blocks / scale).astype(np.float32).astype(dtype).astype(np.float64)
    return np.moveaxis((codes * scale).reshape(v.shape), -1, axis)


WIDE = False


def mx_kscale(k):
    if not WIDE:
        return np.ones(k)
    levels = np.array([10, -10, 5, -5, 0])
    a = np.random.permutation(np.resize(levels, k // 512 * 4)).reshape(k // 512, 4)
    idx = np.arange(k)
    return np.exp2(a[idx // 512, idx % 128 // 32])


BF16 = ml_dtypes.bfloat16


def bf(x):
    return np.asarray(x, np.float32).astype(BF16)


def f64(x):
    return np.asarray(x).astype(np.float64)


N, C = 4096, 512
KS = 3 * C
SQRT3 = np.sqrt(3.0)
EPS = 1e-6


def setup_inputs():
    t = mx_kscale(KS)
    return {"s": bf(np.random.standard_normal((N, C))),
            "v": bf(np.random.standard_normal((N, C, 3))),
            "g_s": bf(np.random.standard_normal((N, KS)) * t),
            "w0": bf(np.random.standard_normal((KS, C)) / t[:, None]),
            "ln_g0": bf(1.0 + 0.1 * np.random.standard_normal(C))}


def reference(s, v, g_s, w0, ln_g0):
    s, v = f64(s), f64(v)
    ss = s * s
    vv0 = np.sum(v * v, axis=-1) / SQRT3
    sc = np.concatenate([s, ss, vv0], axis=-1) * f64(g_s)
    y = s + (mxq(sc, 1, "e4m3") @ mxq(f64(w0), 0, "e4m3")) / np.sqrt(KS)
    mu = np.mean(y, axis=-1, keepdims=True)
    sd = np.sqrt(np.mean((y - mu) ** 2, axis=-1, keepdims=True) + EPS)
    return (y - mu) / sd * f64(ln_g0)

@@ -1,0 +1,224 @@
+import math
+
+import concourse.mybir as mybir
+from concourse.masks import make_identity
+
+F32 = mybir.dt.float32
+BF16 = mybir.dt.bfloat16
+U32 = mybir.dt.uint32
+U8 = mybir.dt.uint8
+FP8X4 = mybir.dt.float8_e4m3fn_x4
+MULT = mybir.AluOpType.mult
+ADD = mybir.AluOpType.add
+SQUARE = mybir.ActivationFunctionType.Square
+SQRT = mybir.ActivationFunctionType.Sqrt
+
+P = 128
+POINTS = 4096
+C = 512
+XYZ = 3
+PASSES = 3
+KS = PASSES * C
+PACK = 4
+HALVES = 2
+PAIR = 2
+WORDS = C // PAIR
+R = 2
+CHUNKS = POINTS // (P * R)
+EPS = 1e-6
+
+FLOPS = 2 * POINTS * KS * C
+
+
+def tile_selfinteraction_pc_t_kernel(tc, s, v, g_s, w0, ln_g0, out):
+    nc = tc.nc
+
+    s_chunks = s.rearrange("(k p r) c -> k p (r c)", p=P, r=R)
+    g_chunks = g_s.rearrange("(k p r) c -> k p (r c)", p=P, r=R)
+    v_chunks = v.rearrange("(k p r) c j -> k p (r c j)", p=P, r=R)
+    out_chunks = out.rearrange("(k p r) c -> k p (r c)", p=P, r=R)
+
+    with tc.tile_pool(name="keep", bufs=1) as keep, tc.tile_pool(name="loads", bufs=3) as loads, tc.tile_pool(
+        name="work", bufs=2
+    ) as work, tc.tile_pool(name="small", bufs=3) as small, tc.psum_pool(name="psum", bufs=2) as psum:
+
+        def load_chunk(k):
+            v_t = loads.tile([P, R * C * XYZ], BF16)
+            nc.sync.dma_start(out=v_t[:], in_=v_chunks[k])
+            s_t = loads.tile([P, R * C], BF16, bufs=5)
+            nc.sync.dma_start(out=s_t[:], in_=s_chunks[k])
+            g_t = loads.tile([P, R * KS], BF16)
+            nc.sync.dma_start(out=g_t[:], in_=g_chunks[k])
+            return s_t, g_t, v_t
+
+        loaded = load_chunk(0)
+
+        ident = keep.tile([P, P], F32)
+        make_identity(nc, ident[:])
+        eps = keep.tile([P, 1], F32)
+        nc.vector.memset(eps[:], EPS)
+
+        w_rows = keep.tile([P, PASSES * PACK * C], BF16)
+        nc.sync.dma_start(
+            out=w_rows[:].rearrange("p (a x) -> p a x", a=PASSES * HALVES),
+            in_=w0.rearrange("(a p e) c -> p a (e c)", a=PASSES * HALVES, p=P, e=PAIR),
+        )
+        gain = keep.tile([P, C], BF16)
+        nc.sync.dma_start(out=gain[:], in_=ln_g0.partition_broadcast(P))
+
+        w_codes = keep.tile([P, PASSES * C], U32, align_bytes=64)
+        w_scales = keep.tile([P, PASSES * C], U8, align_bytes=64)
+        for g in range(PASSES):
+            w_grouped = keep.tile([P, C * PACK], BF16, align_bytes=64, bufs=PASSES)
+            nc.vector.tensor_copy(
+                out=w_grouped[:].rearrange("p (c t) -> p c t", t=PACK),
+                in_=w_rows[:, g * PACK * C : (g + 1) * PACK * C].rearrange("p (t c) -> p c t", t=PACK),
+            )
+            nc.vector.quantize_mx(
+                out=w_codes[:, g * C : (g + 1) * C].bitcast(FP8X4),
+                scales=w_scales[:, g * C : (g + 1) * C],
+                in_=w_grouped[:],
+            )
+
+        for k in range(CHUNKS):
+            s_t, g_t, v_t = loaded
+            if k + 1 < CHUNKS:
+                loaded = load_chunk(k + 1)
+
+            s_rows = s_t[:].rearrange("p (r c) -> p r c", r=R)
+            g_rows = g_t[:].rearrange("p (r g c) -> p r g c", r=R, g=PASSES)
+
+            ss = work.tile([P, R * C], F32)
+            nc.scalar.activation(out=ss[:], in_=s_t[:], func=SQUARE)
+            u01 = work.tile([P, R * 2 * C], BF16)
+            u01_rows = u01[:].rearrange("p (r g c) -> p r g c", r=R, g=2)
+            nc.vector.tensor_tensor(out=u01_rows[:, :, 0, :], in0=s_rows, in1=g_rows[:, :, 0, :], op=MULT)
+            nc.vector.tensor_tensor(
+                out=u01_rows[:, :, 1, :], in0=ss[:].rearrange("p (r c) -> p r c", r=R), in1=g_rows[:, :, 1, :], op=MULT
+            )
+            u01_words = u01[:].bitcast(F32)
+
+            g_words = g_t[:].bitcast(F32)
+            gate_bank = psum.tile([P, R * WORDS], F32)
+            for r in range(R):
+                for h in range(HALVES):
+                    first = (r * PASSES + 2) * WORDS + h * P
+                    nc.tensor.transpose(
+                        gate_bank[:, (r * HALVES + h) * P : (r * HALVES + h + 1) * P],
+                        g_words[:, first : first + P],
+                        ident[:],
+                    )
+            gate_t = work.tile([P, R * WORDS], F32)
+            nc.scalar.copy(
+                out=gate_t[:].rearrange("p (r n h) -> p r n h", r=R, h=HALVES),
+                in_=gate_bank[:].rearrange("p (r h n) -> p r n h", r=R, h=HALVES),
+            )
+            gate_values = gate_t[:].bitcast(BF16)
+
+            y = work.tile([P, R * C], F32)
+            y_sum = small.tile([P, R], F32)
+            for r in range(R):
+                u01_bank = psum.tile([P, 2 * WORDS], F32)
+                for b in range(2 * HALVES):
+                    first = r * 2 * WORDS + b * P
+                    nc.tensor.transpose(u01_bank[:, b * P : (b + 1) * P], u01_words[:, first : first + P], ident[:])
+                u01_grouped = work.tile([P, 2 * WORDS], F32, align_bytes=64)
+                nc.scalar.copy(
+                    out=u01_grouped[:].rearrange("p (g n h) -> p g n h", g=2, h=HALVES),
+                    in_=u01_bank[:].rearrange("p (g h n) -> p g n h", g=2, h=HALVES),
+                )
+
+                v_sq = work.tile([P, C * XYZ], F32)
+                nc.scalar.activation(out=v_sq[:], in_=v_t[:, r * C * XYZ : (r + 1) * C * XYZ], func=SQUARE)
+                v_sq_planes = v_sq[:].rearrange("n (h q e j) -> n h e j q", h=HALVES, q=P, e=PAIR, j=XYZ)
+                vv_bank = psum.tile([P, PACK * P], F32)
+                for h in range(HALVES):
+                    for e in range(PAIR):
+                        t = PAIR * h + e
+                        for j in range(XYZ):
+                            nc.tensor.matmul(
+                                vv_bank[:, t * P : (t + 1) * P],
+                                lhsT=v_sq_planes[:, h, e, j, :],
+                                rhs=ident[:],
+                                is_transpose=True,
+                                start=(j == 0),
+                                stop=(j == XYZ - 1),
+                            )
+                u2_grouped = work.tile([P, C], BF16, align_bytes=64)
+                nc.vector.scalar_tensor_tensor(
+                    out=u2_grouped[:].rearrange("p (n t) -> p n t", t=PACK),
+                    in0=vv_bank[:].rearrange("p (t n) -> p n t", t=PACK),
+                    scalar=1.0 / math.sqrt(3.0),
+                    in1=gate_values[:, r * C : (r + 1) * C].rearrange("p (n t) -> p n t", t=PACK),
+                    op0=MULT,
+                    op1=MULT,
+                )
+
+                u_codes = work.tile([P, PASSES * P], U32, align_bytes=64)
+                u_scales = work.tile([P, PASSES * P], U8, align_bytes=64)
+                nc.vector.quantize_mx(
+                    out=u_codes[:, 0 : 2 * P].bitcast(FP8X4),
+                    scales=u_scales[:, 0 : 2 * P],
+                    in_=u01_grouped[:].bitcast(BF16),
+                )
+                nc.vector.quantize_mx(
+                    out=u_codes[:, 2 * P : 3 * P].bitcast(FP8X4),
+                    scales=u_scales[:, 2 * P : 3 * P],
+                    in_=u2_grouped[:],
+                )
+
+                acc = psum.tile([P, C], F32)
+                for g in range(PASSES):
+                    nc.tensor.matmul_mx(
+                        out=acc[:],
+                        lhsT=u_codes[:, g * P : (g + 1) * P].bitcast(FP8X4),
+                        lhsT_scale=u_scales[:, g * P : (g + 1) * P],
+                        rhs=w_codes[:, g * C : (g + 1) * C].bitcast(FP8X4),
+                        rhs_scale=w_scales[:, g * C : (g + 1) * C],
+                        start=(g == 0),
+                        stop=(g == PASSES - 1),
+                    )
+
+                nc.vector.scalar_tensor_tensor(
+                    out=y[:, r * C : (r + 1) * C],
+                    in0=acc[:],
+                    scalar=1.0 / math.sqrt(KS),
+                    in1=s_t[:, r * C : (r + 1) * C],
+                    op0=MULT,
+                    op1=ADD,
+                    accum_out=y_sum[:, r : r + 1],
+                )
+
+            neg_mean = small.tile([P, R], F32)
+            nc.vector.tensor_scalar(out=neg_mean[:], in0=y_sum[:], scalar1=-1.0 / C, scalar2=None, op0=MULT)
+            sq_sum = small.tile([P, R], F32)
+            centred = work.tile([P, R * C], F32)
+            for r in range(R):
+                cols = slice(r * C, (r + 1) * C)
+                squares = work.tile([P, C], BF16, bufs=4)
+                nc.scalar.activation(
+                    out=squares[:],
+                    in_=y[:, cols],
+                    func=SQUARE,
+                    bias=neg_mean[:, r : r + 1],
+                    accum_out=sq_sum[:, r : r + 1],
+                )
+                nc.vector.scalar_tensor_tensor(
+                    out=centred[:, cols],
+                    in0=y[:, cols],
+                    scalar=neg_mean[:, r : r + 1],
+                    in1=gain[:],
+                    op0=ADD,
+                    op1=MULT,
+                )
+            sd = small.tile([P, R], F32)
+            nc.scalar.activation(out=sd[:], in_=sq_sum[:], func=SQRT, bias=eps[:, 0:1], scale=1.0 / C)
+            inv_sd = small.tile([P, R], F32)
+            nc.vector.reciprocal(out=inv_sd[:], in_=sd[:])
+            result = work.tile([P, R * C], F32, bufs=3)
+            for r in range(R):
+                cols = slice(r * C, (r + 1) * C)
+                nc.vector.tensor_scalar(
+                    out=result[:, cols], in0=centred[:, cols], scalar1=inv_sd[:, r : r + 1], scalar2=None, op0=MULT
+                )
+            nc.sync.dma_start(out=out_chunks[k], in_=result[:])

@@ -40,65 +40,84 @@ def tile_selfinteraction_pc_t_kernel(tc, s, v, g_s, w0, ln_g0, out):
 
     with tc.tile_pool(name="keep", bufs=1) as keep, tc.tile_pool(name="loads", bufs=3) as loads, tc.tile_pool(
         name="work", bufs=2
-    ) as work, tc.tile_pool(name="small", bufs=3) as small, tc.psum_pool(name="psum", bufs=2) as psum:
-
-        def load_chunk(k):
-            v_t = loads.tile([P, R * C * XYZ], BF16)
-            nc.sync.dma_start(out=v_t[:], in_=v_chunks[k])
-            s_t = loads.tile([P, R * C], BF16, bufs=5)
-            nc.sync.dma_start(out=s_t[:], in_=s_chunks[k])
-            g_t = loads.tile([P, R * KS], BF16)
-            nc.sync.dma_start(out=g_t[:], in_=g_chunks[k])
-            return s_t, g_t, v_t
-
-        loaded = load_chunk(0)
+    ) as work, tc.tile_pool(name="small", bufs=3) as small, tc.psum_pool(
+        name="psum", bufs=2
+    ) as psum, tc.manual_schedule():
+        held = {}
 
         ident = keep.tile([P, P], F32)
         make_identity(nc, ident[:])
         eps = keep.tile([P, 1], F32)
         nc.vector.memset(eps[:], EPS)
-
         w_rows = keep.tile([P, PASSES * PACK * C], BF16)
-        nc.sync.dma_start(
-            out=w_rows[:].rearrange("p (a x) -> p a x", a=PASSES * HALVES),
-            in_=w0.rearrange("(a p e) c -> p a (e c)", a=PASSES * HALVES, p=P, e=PAIR),
-        )
         gain = keep.tile([P, C], BF16)
-        nc.sync.dma_start(out=gain[:], in_=ln_g0.partition_broadcast(P))
-
         w_codes = keep.tile([P, PASSES * C], U32, align_bytes=64)
         w_scales = keep.tile([P, PASSES * C], U8, align_bytes=64)
-        for g in range(PASSES):
-            w_grouped = keep.tile([P, C * PACK], BF16, align_bytes=64, bufs=PASSES)
-            nc.vector.tensor_copy(
-                out=w_grouped[:].rearrange("p (c t) -> p c t", t=PACK),
-                in_=w_rows[:, g * PACK * C : (g + 1) * PACK * C].rearrange("p (t c) -> p c t", t=PACK),
+
+        def load_weights():
+            nc.sync.dma_start(
+                out=w_rows[:].rearrange("p (a x) -> p a x", a=PASSES * HALVES),
+                in_=w0.rearrange("(a p e) c -> p a (e c)", a=PASSES * HALVES, p=P, e=PAIR),
             )
-            nc.vector.quantize_mx(
-                out=w_codes[:, g * C : (g + 1) * C].bitcast(FP8X4),
-                scales=w_scales[:, g * C : (g + 1) * C],
-                in_=w_grouped[:],
-            )
+            nc.sync.dma_start(out=gain[:], in_=ln_g0.partition_broadcast(P))
 
-        for k in range(CHUNKS):
-            s_t, g_t, v_t = loaded
-            if k + 1 < CHUNKS:
-                loaded = load_chunk(k + 1)
+        def quantise_weights():
+            grouped = []
+            for g in range(PASSES):
+                w_grouped = keep.tile([P, C * PACK], BF16, align_bytes=64, bufs=PASSES)
+                nc.vector.tensor_copy(
+                    out=w_grouped[:].rearrange("p (c t) -> p c t", t=PACK),
+                    in_=w_rows[:, g * PACK * C : (g + 1) * PACK * C].rearrange("p (t c) -> p c t", t=PACK),
+                )
+                grouped.append(w_grouped)
+            for g in range(PASSES):
+                nc.vector.quantize_mx(
+                    out=w_codes[:, g * C : (g + 1) * C].bitcast(FP8X4),
+                    scales=w_scales[:, g * C : (g + 1) * C],
+                    in_=grouped[g][:],
+                )
 
-            s_rows = s_t[:].rearrange("p (r c) -> p r c", r=R)
-            g_rows = g_t[:].rearrange("p (r g c) -> p r g c", r=R, g=PASSES)
+        def load(c):
+            s_t = loads.tile([P, R * C], BF16, bufs=5)
+            nc.sync.dma_start(out=s_t[:], in_=s_chunks[c])
+            v_t = loads.tile([P, R * C * XYZ], BF16)
+            nc.sync.dma_start(out=v_t[:], in_=v_chunks[c])
+            g_t = loads.tile([P, R * KS], BF16)
+            nc.sync.dma_start(out=g_t[:], in_=g_chunks[c])
+            held["s", c], held["v", c], held["g", c] = s_t, v_t, g_t
 
+        def square_s(c):
             ss = work.tile([P, R * C], F32)
-            nc.scalar.activation(out=ss[:], in_=s_t[:], func=SQUARE)
+            nc.scalar.activation(out=ss[:], in_=held["s", c][:], func=SQUARE)
+            held["ss", c] = ss
+
+        def gate_products(c):
+            g_rows = held["g", c][:].rearrange("p (r g c) -> p r g c", r=R, g=PASSES)
             u01 = work.tile([P, R * 2 * C], BF16)
             u01_rows = u01[:].rearrange("p (r g c) -> p r g c", r=R, g=2)
-            nc.vector.tensor_tensor(out=u01_rows[:, :, 0, :], in0=s_rows, in1=g_rows[:, :, 0, :], op=MULT)
             nc.vector.tensor_tensor(
-                out=u01_rows[:, :, 1, :], in0=ss[:].rearrange("p (r c) -> p r c", r=R), in1=g_rows[:, :, 1, :], op=MULT
+                out=u01_rows[:, :, 0, :],
+                in0=held["s", c][:].rearrange("p (r c) -> p r c", r=R),
+                in1=g_rows[:, :, 0, :],
+                op=MULT,
             )
-            u01_words = u01[:].bitcast(F32)
+            nc.vector.tensor_tensor(
+                out=u01_rows[:, :, 1, :],
+                in0=held["ss", c][:].rearrange("p (r c) -> p r c", r=R),
+                in1=g_rows[:, :, 1, :],
+                op=MULT,
+            )
+            held["u01", c] = u01
 
-            g_words = g_t[:].bitcast(F32)
+        def square_v(c):
+            for r in range(R):
+                v_sq = work.tile([P, C * XYZ], F32)
+                nc.scalar.activation(out=v_sq[:], in_=held["v", c][:, r * C * XYZ : (r + 1) * C * XYZ], func=SQUARE)
+                held["v_sq", c, r] = v_sq
+
+        def transpose_words(c):
+            g_words = held["g", c][:].bitcast(F32)
+            u01_words = held["u01", c][:].bitcast(F32)
             gate_bank = psum.tile([P, R * WORDS], F32)
             for r in range(R):
                 for h in range(HALVES):
@@ -108,29 +127,31 @@ def tile_selfinteraction_pc_t_kernel(tc, s, v, g_s, w0, ln_g0, out):
                         g_words[:, first : first + P],
                         ident[:],
                     )
-            gate_t = work.tile([P, R * WORDS], F32)
-            nc.scalar.copy(
-                out=gate_t[:].rearrange("p (r n h) -> p r n h", r=R, h=HALVES),
-                in_=gate_bank[:].rearrange("p (r h n) -> p r n h", r=R, h=HALVES),
-            )
-            gate_values = gate_t[:].bitcast(BF16)
-
-            y = work.tile([P, R * C], F32)
-            y_sum = small.tile([P, R], F32)
+            banks = []
             for r in range(R):
                 u01_bank = psum.tile([P, 2 * WORDS], F32)
                 for b in range(2 * HALVES):
                     first = r * 2 * WORDS + b * P
                     nc.tensor.transpose(u01_bank[:, b * P : (b + 1) * P], u01_words[:, first : first + P], ident[:])
-                u01_grouped = work.tile([P, 2 * WORDS], F32, align_bytes=64)
+                banks.append(u01_bank)
+            gate_t = work.tile([P, R * WORDS], F32)
+            nc.scalar.copy(
+                out=gate_t[:].rearrange("p (r n h) -> p r n h", r=R, h=HALVES),
+                in_=gate_bank[:].rearrange("p (r h n) -> p r n h", r=R, h=HALVES),
+            )
+            u01_grouped = work.tile([P, R * 2 * WORDS], F32, align_bytes=64)
+            for r in range(R):
                 nc.scalar.copy(
-                    out=u01_grouped[:].rearrange("p (g n h) -> p g n h", g=2, h=HALVES),
-                    in_=u01_bank[:].rearrange("p (g h n) -> p g n h", g=2, h=HALVES),
+                    out=u01_grouped[:, r * 2 * WORDS : (r + 1) * 2 * WORDS].rearrange(
+                        "p (g n h) -> p g n h", g=2, h=HALVES
+                    ),
+                    in_=banks[r][:].rearrange("p (g h n) -> p g n h", g=2, h=HALVES),
                 )
+            held["gate_t", c], held["u01_grouped", c] = gate_t, u01_grouped
 
-                v_sq = work.tile([P, C * XYZ], F32)
-                nc.scalar.activation(out=v_sq[:], in_=v_t[:, r * C * XYZ : (r + 1) * C * XYZ], func=SQUARE)
-                v_sq_planes = v_sq[:].rearrange("n (h q e j) -> n h e j q", h=HALVES, q=P, e=PAIR, j=XYZ)
+        def sum_squares(c):
+            for r in range(R):
+                planes = held["v_sq", c, r][:].rearrange("n (h q e j) -> n h e j q", h=HALVES, q=P, e=PAIR, j=XYZ)
                 vv_bank = psum.tile([P, PACK * P], F32)
                 for h in range(HALVES):
                     for e in range(PAIR):
@@ -138,64 +159,85 @@ def tile_selfinteraction_pc_t_kernel(tc, s, v, g_s, w0, ln_g0, out):
                         for j in range(XYZ):
                             nc.tensor.matmul(
                                 vv_bank[:, t * P : (t + 1) * P],
-                                lhsT=v_sq_planes[:, h, e, j, :],
+                                lhsT=planes[:, h, e, j, :],
                                 rhs=ident[:],
                                 is_transpose=True,
                                 start=(j == 0),
                                 stop=(j == XYZ - 1),
                             )
-                u2_grouped = work.tile([P, C], BF16, align_bytes=64)
+                held["vv", c, r] = vv_bank
+
+        def quantise_01(c):
+            codes01 = work.tile([P, R * 2 * P], U32, align_bytes=64)
+            scales01 = work.tile([P, R * 2 * P], U8, align_bytes=64)
+            nc.vector.quantize_mx(
+                out=codes01[:].bitcast(FP8X4), scales=scales01[:], in_=held["u01_grouped", c][:].bitcast(BF16)
+            )
+            held["codes01", c], held["scales01", c] = codes01, scales01
+
+        def gate_vv(c):
+            gate_values = held["gate_t", c][:].bitcast(BF16)
+            u2_grouped = work.tile([P, R * C], BF16, align_bytes=64)
+            for r in range(R):
                 nc.vector.scalar_tensor_tensor(
-                    out=u2_grouped[:].rearrange("p (n t) -> p n t", t=PACK),
-                    in0=vv_bank[:].rearrange("p (t n) -> p n t", t=PACK),
+                    out=u2_grouped[:, r * C : (r + 1) * C].rearrange("p (n t) -> p n t", t=PACK),
+                    in0=held["vv", c, r][:].rearrange("p (t n) -> p n t", t=PACK),
                     scalar=1.0 / math.sqrt(3.0),
                     in1=gate_values[:, r * C : (r + 1) * C].rearrange("p (n t) -> p n t", t=PACK),
                     op0=MULT,
                     op1=MULT,
                 )
+            held["u2_grouped", c] = u2_grouped
 
-                u_codes = work.tile([P, PASSES * P], U32, align_bytes=64)
-                u_scales = work.tile([P, PASSES * P], U8, align_bytes=64)
-                nc.vector.quantize_mx(
-                    out=u_codes[:, 0 : 2 * P].bitcast(FP8X4),
-                    scales=u_scales[:, 0 : 2 * P],
-                    in_=u01_grouped[:].bitcast(BF16),
-                )
-                nc.vector.quantize_mx(
-                    out=u_codes[:, 2 * P : 3 * P].bitcast(FP8X4),
-                    scales=u_scales[:, 2 * P : 3 * P],
-                    in_=u2_grouped[:],
-                )
+        def quantise_2(c):
+            codes2 = work.tile([P, R * P], U32, align_bytes=64)
+            scales2 = work.tile([P, R * P], U8, align_bytes=64)
+            nc.vector.quantize_mx(out=codes2[:].bitcast(FP8X4), scales=scales2[:], in_=held["u2_grouped", c][:])
+            held["codes2", c], held["scales2", c] = codes2, scales2
 
+        def multiply(c):
+            for r in range(R):
                 acc = psum.tile([P, C], F32)
                 for g in range(PASSES):
+                    if g < 2:
+                        codes, scales, first = held["codes01", c], held["scales01", c], (r * 2 + g) * P
+                    else:
+                        codes, scales, first = held["codes2", c], held["scales2", c], r * P
                     nc.tensor.matmul_mx(
                         out=acc[:],
-                        lhsT=u_codes[:, g * P : (g + 1) * P].bitcast(FP8X4),
-                        lhsT_scale=u_scales[:, g * P : (g + 1) * P],
+                        lhsT=codes[:, first : first + P].bitcast(FP8X4),
+                        lhsT_scale=scales[:, first : first + P],
                         rhs=w_codes[:, g * C : (g + 1) * C].bitcast(FP8X4),
                         rhs_scale=w_scales[:, g * C : (g + 1) * C],
                         start=(g == 0),
                         stop=(g == PASSES - 1),
                     )
+                held["acc", c, r] = acc
 
+        def residual(c):
+            y = work.tile([P, R * C], F32)
+            y_sum = small.tile([P, R], F32)
+            for r in range(R):
                 nc.vector.scalar_tensor_tensor(
                     out=y[:, r * C : (r + 1) * C],
-                    in0=acc[:],
+                    in0=held["acc", c, r][:],
                     scalar=1.0 / math.sqrt(KS),
-                    in1=s_t[:, r * C : (r + 1) * C],
+                    in1=held["s", c][:, r * C : (r + 1) * C],
                     op0=MULT,
                     op1=ADD,
                     accum_out=y_sum[:, r : r + 1],
                 )
-
             neg_mean = small.tile([P, R], F32)
             nc.vector.tensor_scalar(out=neg_mean[:], in0=y_sum[:], scalar1=-1.0 / C, scalar2=None, op0=MULT)
+            held["y", c], held["neg_mean", c] = y, neg_mean
+
+        def centre(c):
+            y, neg_mean = held["y", c], held["neg_mean", c]
             sq_sum = small.tile([P, R], F32)
             centred = work.tile([P, R * C], F32)
             for r in range(R):
                 cols = slice(r * C, (r + 1) * C)
-                squares = work.tile([P, C], BF16, bufs=4)
+                squares = work.tile([P, C], BF16)
                 nc.scalar.activation(
                     out=squares[:],
                     in_=y[:, cols],
@@ -211,14 +253,53 @@ def tile_selfinteraction_pc_t_kernel(tc, s, v, g_s, w0, ln_g0, out):
                     op0=ADD,
                     op1=MULT,
                 )
+            held["sq_sum", c], held["centred", c] = sq_sum, centred
+
+        def deviation(c):
             sd = small.tile([P, R], F32)
-            nc.scalar.activation(out=sd[:], in_=sq_sum[:], func=SQRT, bias=eps[:, 0:1], scale=1.0 / C)
+            nc.scalar.activation(out=sd[:], in_=held["sq_sum", c][:], func=SQRT, bias=eps[:, 0:1], scale=1.0 / C)
             inv_sd = small.tile([P, R], F32)
             nc.vector.reciprocal(out=inv_sd[:], in_=sd[:])
+            held["inv_sd", c] = inv_sd
+
+        def scale_and_store(c):
             result = work.tile([P, R * C], F32, bufs=3)
             for r in range(R):
                 cols = slice(r * C, (r + 1) * C)
                 nc.vector.tensor_scalar(
-                    out=result[:, cols], in0=centred[:, cols], scalar1=inv_sd[:, r : r + 1], scalar2=None, op0=MULT
+                    out=result[:, cols],
+                    in0=held["centred", c][:, cols],
+                    scalar1=held["inv_sd", c][:, r : r + 1],
+                    scalar2=None,
+                    op0=MULT,
                 )
-            nc.sync.dma_start(out=out_chunks[k], in_=result[:])
+            nc.sync.dma_start(out=out_chunks[c], in_=result[:])
+
+        def run(stage, c):
+            if 0 <= c < CHUNKS:
+                stage(c)
+
+        def step(i):
+            run(transpose_words, i)
+            run(sum_squares, i)
+            run(gate_products, i + 1)
+            run(centre, i - 2)
+            run(quantise_01, i)
+            run(gate_vv, i)
+            run(deviation, i - 2)
+            run(scale_and_store, i - 2)
+            run(quantise_2, i)
+            run(square_v, i + 1)
+            run(multiply, i - 1)
+            run(residual, i - 1)
+            run(square_s, i + 2)
+            run(load, i + 3)
+
+        step(-3)
+        step(-2)
+        load_weights()
+        step(-1)
+        step(0)
+        quantise_weights()
+        for i in range(1, CHUNKS + 2):
+            step(i)

@@ -88,7 +88,9 @@ def tile_selfinteraction_pc_t_kernel(tc, s, v, g_s, w0, ln_g0, out):
 
         def square_s(c):
             ss = work.tile([P, R * C], F32)
-            nc.scalar.activation(out=ss[:], in_=held["s", c][:], func=SQUARE)
+            for r in range(R):
+                cols = slice(r * C, (r + 1) * C)
+                nc.gpsimd.tensor_tensor(out=ss[:, cols], in0=held["s", c][:, cols], in1=held["s", c][:, cols], op=MULT)
             held["ss", c] = ss
 
         def gate_products(c):

@@ -88,9 +88,7 @@ def tile_selfinteraction_pc_t_kernel(tc, s, v, g_s, w0, ln_g0, out):
 
         def square_s(c):
             ss = work.tile([P, R * C], F32)
-            for r in range(R):
-                cols = slice(r * C, (r + 1) * C)
-                nc.gpsimd.tensor_tensor(out=ss[:, cols], in0=held["s", c][:, cols], in1=held["s", c][:, cols], op=MULT)
+            nc.scalar.activation(out=ss[:], in_=held["s", c][:], func=SQUARE)
             held["ss", c] = ss
 
         def gate_products(c):
@@ -136,11 +134,6 @@ def tile_selfinteraction_pc_t_kernel(tc, s, v, g_s, w0, ln_g0, out):
                     first = r * 2 * WORDS + b * P
                     nc.tensor.transpose(u01_bank[:, b * P : (b + 1) * P], u01_words[:, first : first + P], ident[:])
                 banks.append(u01_bank)
-            gate_t = work.tile([P, R * WORDS], F32)
-            nc.scalar.copy(
-                out=gate_t[:].rearrange("p (r n h) -> p r n h", r=R, h=HALVES),
-                in_=gate_bank[:].rearrange("p (r h n) -> p r n h", r=R, h=HALVES),
-            )
             u01_grouped = work.tile([P, R * 2 * WORDS], F32, align_bytes=64)
             for r in range(R):
                 nc.scalar.copy(
@@ -149,7 +142,7 @@ def tile_selfinteraction_pc_t_kernel(tc, s, v, g_s, w0, ln_g0, out):
                     ),
                     in_=banks[r][:].rearrange("p (g h n) -> p g n h", g=2, h=HALVES),
                 )
-            held["gate_t", c], held["u01_grouped", c] = gate_t, u01_grouped
+            held["gate_bank", c], held["u01_grouped", c] = gate_bank, u01_grouped
 
         def sum_squares(c):
             for r in range(R):
@@ -178,7 +171,12 @@ def tile_selfinteraction_pc_t_kernel(tc, s, v, g_s, w0, ln_g0, out):
             held["codes01", c], held["scales01", c] = codes01, scales01
 
         def gate_vv(c):
-            gate_values = held["gate_t", c][:].bitcast(BF16)
+            gate_t = work.tile([P, R * WORDS], F32)
+            nc.vector.tensor_copy(
+                out=gate_t[:].rearrange("p (r n h) -> p r n h", r=R, h=HALVES),
+                in_=held["gate_bank", c][:].rearrange("p (r h n) -> p r n h", r=R, h=HALVES),
+            )
+            gate_values = gate_t[:].bitcast(BF16)
             u2_grouped = work.tile([P, R * C], BF16, align_bytes=64)
             for r in range(R):
                 nc.vector.scalar_tensor_tensor(

import math

import concourse.mybir as mybir
from concourse.masks import make_identity

F32 = mybir.dt.float32
BF16 = mybir.dt.bfloat16
U32 = mybir.dt.uint32
U8 = mybir.dt.uint8
FP8X4 = mybir.dt.float8_e4m3fn_x4
MULT = mybir.AluOpType.mult
ADD = mybir.AluOpType.add
SQUARE = mybir.ActivationFunctionType.Square
SQRT = mybir.ActivationFunctionType.Sqrt

P = 128
POINTS = 4096
C = 512
XYZ = 3
PASSES = 3
KS = PASSES * C
PACK = 4
HALVES = 2
PAIR = 2
WORDS = C // PAIR
R = 2
CHUNKS = POINTS // (P * R)
EPS = 1e-6

FLOPS = 2 * POINTS * KS * C


def tile_selfinteraction_pc_t_kernel(tc, s, v, g_s, w0, ln_g0, out):
    nc = tc.nc

    s_chunks = s.rearrange("(k p r) c -> k p (r c)", p=P, r=R)
    g_chunks = g_s.rearrange("(k p r) c -> k p (r c)", p=P, r=R)
    v_chunks = v.rearrange("(k p r) c j -> k p (r c j)", p=P, r=R)
    out_chunks = out.rearrange("(k p r) c -> k p (r c)", p=P, r=R)

    with tc.tile_pool(name="keep", bufs=1) as keep, tc.tile_pool(name="loads", bufs=3) as loads, tc.tile_pool(
        name="work", bufs=2
    ) as work, tc.tile_pool(name="small", bufs=3) as small, tc.psum_pool(
        name="psum", bufs=2
    ) as psum, tc.manual_schedule():
        held = {}

        ident = keep.tile([P, P], F32)
        make_identity(nc, ident[:])
        eps = keep.tile([P, 1], F32)
        nc.vector.memset(eps[:], EPS)
        w_rows = keep.tile([P, PASSES * PACK * C], BF16)
        gain = keep.tile([P, C], BF16)
        w_codes = keep.tile([P, PASSES * C], U32, align_bytes=64)
        w_scales = keep.tile([P, PASSES * C], U8, align_bytes=64)

        def load_weights():
            nc.sync.dma_start(
                out=w_rows[:].rearrange("p (a x) -> p a x", a=PASSES * HALVES),
                in_=w0.rearrange("(a p e) c -> p a (e c)", a=PASSES * HALVES, p=P, e=PAIR),
            )
            nc.sync.dma_start(out=gain[:], in_=ln_g0.partition_broadcast(P))

        def quantise_weights():
            grouped = []
            for g in range(PASSES):
                w_grouped = keep.tile([P, C * PACK], BF16, align_bytes=64, bufs=PASSES)
                nc.vector.tensor_copy(
                    out=w_grouped[:].rearrange("p (c t) -> p c t", t=PACK),
                    in_=w_rows[:, g * PACK * C : (g + 1) * PACK * C].rearrange("p (t c) -> p c t", t=PACK),
                )
                grouped.append(w_grouped)
            for g in range(PASSES):
                nc.vector.quantize_mx(
                    out=w_codes[:, g * C : (g + 1) * C].bitcast(FP8X4),
                    scales=w_scales[:, g * C : (g + 1) * C],
                    in_=grouped[g][:],
                )

        def load(c):
            s_t = loads.tile([P, R * C], BF16, bufs=5)
            nc.sync.dma_start(out=s_t[:], in_=s_chunks[c])
            v_t = loads.tile([P, R * C * XYZ], BF16)
            nc.sync.dma_start(out=v_t[:], in_=v_chunks[c])
            g_t = loads.tile([P, R * KS], BF16)
            nc.sync.dma_start(out=g_t[:], in_=g_chunks[c])
            held["s", c], held["v", c], held["g", c] = s_t, v_t, g_t

        def square_s(c):
            ss = work.tile([P, R * C], F32)
            nc.scalar.activation(out=ss[:], in_=held["s", c][:], func=SQUARE)
            held["ss", c] = ss

        def gate_products(c):
            g_rows = held["g", c][:].rearrange("p (r g c) -> p r g c", r=R, g=PASSES)
            u01 = work.tile([P, R * 2 * C], BF16)
            u01_rows = u01[:].rearrange("p (r g c) -> p r g c", r=R, g=2)
            nc.vector.tensor_tensor(
                out=u01_rows[:, :, 0, :],
                in0=held["s", c][:].rearrange("p (r c) -> p r c", r=R),
                in1=g_rows[:, :, 0, :],
                op=MULT,
            )
            nc.vector.tensor_tensor(
                out=u01_rows[:, :, 1, :],
                in0=held["ss", c][:].rearrange("p (r c) -> p r c", r=R),
                in1=g_rows[:, :, 1, :],
                op=MULT,
            )
            held["u01", c] = u01

        def square_v(c):
            for r in range(R):
                v_sq = work.tile([P, C * XYZ], F32)
                nc.scalar.activation(out=v_sq[:], in_=held["v", c][:, r * C * XYZ : (r + 1) * C * XYZ], func=SQUARE)
                held["v_sq", c, r] = v_sq

        def transpose_words(c):
            g_words = held["g", c][:].bitcast(F32)
            u01_words = held["u01", c][:].bitcast(F32)
            gate_bank = psum.tile([P, R * WORDS], F32)
            for r in range(R):
                for h in range(HALVES):
                    first = (r * PASSES + 2) * WORDS + h * P
                    nc.tensor.transpose(
                        gate_bank[:, (r * HALVES + h) * P : (r * HALVES + h + 1) * P],
                        g_words[:, first : first + P],
                        ident[:],
                    )
            banks = []
            for r in range(R):
                u01_bank = psum.tile([P, 2 * WORDS], F32)
                for b in range(2 * HALVES):
                    first = r * 2 * WORDS + b * P
                    nc.tensor.transpose(u01_bank[:, b * P : (b + 1) * P], u01_words[:, first : first + P], ident[:])
                banks.append(u01_bank)
            u01_grouped = work.tile([P, R * 2 * WORDS], F32, align_bytes=64)
            for r in range(R):
                nc.scalar.copy(
                    out=u01_grouped[:, r * 2 * WORDS : (r + 1) * 2 * WORDS].rearrange(
                        "p (g n h) -> p g n h", g=2, h=HALVES
                    ),
                    in_=banks[r][:].rearrange("p (g h n) -> p g n h", g=2, h=HALVES),
                )
            held["gate_bank", c], held["u01_grouped", c] = gate_bank, u01_grouped

        def sum_squares(c):
            for r in range(R):
                planes = held["v_sq", c, r][:].rearrange("n (h q e j) -> n h e j q", h=HALVES, q=P, e=PAIR, j=XYZ)
                vv_bank = psum.tile([P, PACK * P], F32)
                for h in range(HALVES):
                    for e in range(PAIR):
                        t = PAIR * h + e
                        for j in range(XYZ):
                            nc.tensor.matmul(
                                vv_bank[:, t * P : (t + 1) * P],
                                lhsT=planes[:, h, e, j, :],
                                rhs=ident[:],
                                is_transpose=True,
                                start=(j == 0),
                                stop=(j == XYZ - 1),
                            )
                held["vv", c, r] = vv_bank

        def quantise_01(c):
            codes01 = work.tile([P, R * 2 * P], U32, align_bytes=64)
            scales01 = work.tile([P, R * 2 * P], U8, align_bytes=64)
            nc.vector.quantize_mx(
                out=codes01[:].bitcast(FP8X4), scales=scales01[:], in_=held["u01_grouped", c][:].bitcast(BF16)
            )
            held["codes01", c], held["scales01", c] = codes01, scales01

        def gate_vv(c):
            gate_t = work.tile([P, R * WORDS], F32)
            nc.vector.tensor_copy(
                out=gate_t[:].rearrange("p (r n h) -> p r n h", r=R, h=HALVES),
                in_=held["gate_bank", c][:].rearrange("p (r h n) -> p r n h", r=R, h=HALVES),
            )
            gate_values = gate_t[:].bitcast(BF16)
            u2_grouped = work.tile([P, R * C], BF16, align_bytes=64)
            for r in range(R):
                nc.vector.scalar_tensor_tensor(
                    out=u2_grouped[:, r * C : (r + 1) * C].rearrange("p (n t) -> p n t", t=PACK),
                    in0=held["vv", c, r][:].rearrange("p (t n) -> p n t", t=PACK),
                    scalar=1.0 / math.sqrt(3.0),
                    in1=gate_values[:, r * C : (r + 1) * C].rearrange("p (n t) -> p n t", t=PACK),
                    op0=MULT,
                    op1=MULT,
                )
            held["u2_grouped", c] = u2_grouped

        def quantise_2(c):
            codes2 = work.tile([P, R * P], U32, align_bytes=64)
            scales2 = work.tile([P, R * P], U8, align_bytes=64)
            nc.vector.quantize_mx(out=codes2[:].bitcast(FP8X4), scales=scales2[:], in_=held["u2_grouped", c][:])
            held["codes2", c], held["scales2", c] = codes2, scales2

        def multiply(c):
            for r in range(R):
                acc = psum.tile([P, C], F32)
                for g in range(PASSES):
                    if g < 2:
                        codes, scales, first = held["codes01", c], held["scales01", c], (r * 2 + g) * P
                    else:
                        codes, scales, first = held["codes2", c], held["scales2", c], r * P
                    nc.tensor.matmul_mx(
                        out=acc[:],
                        lhsT=codes[:, first : first + P].bitcast(FP8X4),
                        lhsT_scale=scales[:, first : first + P],
                        rhs=w_codes[:, g * C : (g + 1) * C].bitcast(FP8X4),
                        rhs_scale=w_scales[:, g * C : (g + 1) * C],
                        start=(g == 0),
                        stop=(g == PASSES - 1),
                    )
                held["acc", c, r] = acc

        def residual(c):
            y = work.tile([P, R * C], F32)
            y_sum = small.tile([P, R], F32)
            for r in range(R):
                nc.vector.scalar_tensor_tensor(
                    out=y[:, r * C : (r + 1) * C],
                    in0=held["acc", c, r][:],
                    scalar=1.0 / math.sqrt(KS),
                    in1=held["s", c][:, r * C : (r + 1) * C],
                    op0=MULT,
                    op1=ADD,
                    accum_out=y_sum[:, r : r + 1],
                )
            neg_mean = small.tile([P, R], F32)
            nc.vector.tensor_scalar(out=neg_mean[:], in0=y_sum[:], scalar1=-1.0 / C, scalar2=None, op0=MULT)
            held["y", c], held["neg_mean", c] = y, neg_mean

        def centre(c):
            y, neg_mean = held["y", c], held["neg_mean", c]
            sq_sum = small.tile([P, R], F32)
            centred = work.tile([P, R * C], F32)
            for r in range(R):
                cols = slice(r * C, (r + 1) * C)
                squares = work.tile([P, C], BF16)
                nc.scalar.activation(
                    out=squares[:],
                    in_=y[:, cols],
                    func=SQUARE,
                    bias=neg_mean[:, r : r + 1],
                    accum_out=sq_sum[:, r : r + 1],
                )
                nc.vector.scalar_tensor_tensor(
                    out=centred[:, cols],
                    in0=y[:, cols],
                    scalar=neg_mean[:, r : r + 1],
                    in1=gain[:],
                    op0=ADD,
                    op1=MULT,
                )
            held["sq_sum", c], held["centred", c] = sq_sum, centred

        def deviation(c):
            sd = small.tile([P, R], F32)
            nc.scalar.activation(out=sd[:], in_=held["sq_sum", c][:], func=SQRT, bias=eps[:, 0:1], scale=1.0 / C)
            inv_sd = small.tile([P, R], F32)
            nc.vector.reciprocal(out=inv_sd[:], in_=sd[:])
            held["inv_sd", c] = inv_sd

        def scale_and_store(c):
            result = work.tile([P, R * C], F32, bufs=3)
            for r in range(R):
                cols = slice(r * C, (r + 1) * C)
                nc.vector.tensor_scalar(
                    out=result[:, cols],
                    in0=held["centred", c][:, cols],
                    scalar1=held["inv_sd", c][:, r : r + 1],
                    scalar2=None,
                    op0=MULT,
                )
            nc.sync.dma_start(out=out_chunks[c], in_=result[:])

        def run(stage, c):
            if 0 <= c < CHUNKS:
                stage(c)

        def step(i):
            run(transpose_words, i)
            run(sum_squares, i)
            run(gate_products, i + 1)
            run(centre, i - 2)
            run(quantise_01, i)
            run(gate_vv, i)
            run(deviation, i - 2)
            run(scale_and_store, i - 2)
            run(quantise_2, i)
            run(square_v, i + 1)
            run(multiply, i - 1)
            run(residual, i - 1)
            run(square_s, i + 2)
            run(load, i + 3)

        step(-3)
        step(-2)
        load_weights()
        step(-1)
        step(0)
        quantise_weights()
        for i in range(1, CHUNKS + 2):
            step(i)
